import numpy as np
import ml_dtypes


def mxq(x, axis, fmt="e4m3"):
    dtype, down = {"e4m3": (ml_dtypes.float8_e4m3fn, 7), "e5m2": (ml_dtypes.float8_e5m2, 14)}[fmt]
    v = np.moveaxis(np.asarray(x, np.float32).astype(ml_dtypes.bfloat16).astype(np.float64), axis, -1)
    blocks = v.reshape(v.shape[:-1] + (-1, 32))
    amax = np.abs(blocks).max(-1, keepdims=True)
    byte = np.maximum(np.where(amax > 0, np.frexp(amax)[1] - 1 + 127, 0) - down, 1)
    scale = np.exp2(byte - 127.0)
    codes = (blocks / scale).astype(np.float32).astype(dtype).astype(np.float64)
    return np.moveaxis((codes * scale).reshape(v.shape), -1, axis)


WIDE = False


def mx_kscale(k):
    if not WIDE:
        return np.ones(k)
    levels = np.array([10, -10, 5, -5, 0])
    if k % 512:
        return np.exp2(np.random.permutation(np.resize(levels, k // 32))).repeat(32)
    a = np.empty((k // 512, 16))
    for p in range(k // 512):
        a[p, :8] = np.random.permutation(np.resize(levels, 8))
        for g in range(8):
            far = levels[np.abs(levels - a[p, g]) >= 10]
            a[p, g + 8] = far[np.random.randint(len(far))]
    return np.exp2(a.ravel()).repeat(32)


BF16 = ml_dtypes.bfloat16


def bf(x):
    return np.asarray(x, np.float32).astype(BF16)


def f64(x):
    return np.asarray(x).astype(np.float64)


E2M1 = np.array([0.0, 0.5, 1.0, 1.5, 2.0, 3.0, 4.0, 6.0, -0.0, -0.5, -1.0, -1.5, -2.0, -3.0, -4.0, -6.0])


def pack_weight(w, fmt):
    k, n = w.shape
    w = f64(bf(w)).reshape(k // 32, 32, n)
    amax = np.abs(w).max(1)
    if fmt == "e4m3":
        byte = np.frexp(amax)[1] - 1 + 127 - 7
    else:
        mant, ex = np.frexp(amax / 6.0)
        byte = np.where(mant > 0.5, ex, ex - 1) + 127
    byte = np.clip(np.where(amax > 0, byte, 1), 1, 254)
    scaled = (w * np.exp2(127.0 - byte)[:, None, :]).reshape(k, n).astype(np.float32)
    by_word = np.ascontiguousarray(scaled.reshape(k // 512, 128, 4, n).transpose(0, 1, 3, 2))
    if fmt == "e4m3":
        words = by_word.astype(ml_dtypes.float8_e4m3fn).view(np.uint8)
    else:
        c = by_word.astype(ml_dtypes.float4_e2m1fn).view(np.uint8) & 0xF
        words = c[..., 0::2] | (c[..., 1::2] << 4)
    return np.ascontiguousarray(words), np.ascontiguousarray(byte.astype(np.uint8).reshape(k // 512, 16, n))


def unpack_weight(words, scales, fmt):
    g, p, n, _ = words.shape
    if fmt == "e4m3":
        vals = np.ascontiguousarray(words).view(ml_dtypes.float8_e4m3fn).astype(np.float64)
    else:
        nib = np.empty((g, p, n, 4), np.uint8)
        nib[..., 0::2] = words & 0xF
        nib[..., 1::2] = words >> 4
        vals = E2M1[nib]
    vals = vals * np.repeat(np.exp2(scales.astype(np.float64) - 127.0), 8, axis=1)[..., None]
    return vals.transpose(0, 1, 3, 2).reshape(g * 512, n)
def pack4(w):
    words, scales = pack_weight(w, "e2m1")
    return words.reshape(words.shape[0], 128, -1), scales


def unpack4(words, scales):
    return unpack_weight(words.reshape(words.shape[0], 128, -1, 2), scales, "e2m1")


B, S, HID, NH, NOPE, ROPE, VD, KV_RANK, SW, QB = 1, 8192, 512, 2, 64, 128, 128, 512, 384, 128


def rotate_half(x):
    h = x.shape[-1] // 2
    return np.concatenate([-x[..., h:], x[..., :h]], axis=-1)


def rope_tables():
    pos = np.arange(S, dtype=np.float64)
    inv = 1.0 / (10000.0 ** (np.arange(0, ROPE, 2, dtype=np.float64) / ROPE))
    ang = pos[:, None] * inv[None, :]
    ang = np.concatenate([ang, ang], axis=-1)
    return bf(np.broadcast_to(np.cos(ang)[None], (B, S, ROPE))), bf(np.broadcast_to(np.sin(ang)[None], (B, S, ROPE)))


def draw0():
    s, t = mx_kscale(HID), mx_kscale(KV_RANK)
    col = np.concatenate([t, np.ones(ROPE)])
    cos, sin = rope_tables()
    hidden_states = bf(np.random.standard_normal((B, S, HID)) * s)
    Wkva_words, Wkva_scales = pack4(np.random.standard_normal((HID, KV_RANK + ROPE)) / np.sqrt(HID) / s[:, None] * col)
    bkva = bf(np.random.standard_normal(KV_RANK + ROPE) * 0.1 * col)
    Wkvb_words, Wkvb_scales = pack4(np.random.standard_normal((KV_RANK, NH * (NOPE + VD))) / np.sqrt(KV_RANK) / t[:, None])
    return {"hidden_states": hidden_states, "cos": cos, "sin": sin,
            "Wkva_words": Wkva_words, "Wkva_scales": Wkva_scales,
            "bkva": bkva,
            "Wkvb_words": Wkvb_words, "Wkvb_scales": Wkvb_scales}


def core(hidden_states, cos, sin, Wkva_words, Wkva_scales, bkva, Wkvb_words, Wkvb_scales):
    ckv = (mxq(f64(hidden_states), 2, "e4m3") @ unpack4(Wkva_words, Wkva_scales)) + f64(bkva)
    kv_lat, k_rope = ckv[..., :KV_RANK], ckv[..., KV_RANK:]
    kv = (mxq(kv_lat, 2, "e4m3") @ unpack4(Wkvb_words, Wkvb_scales)).reshape(B, S, NH, NOPE + VD).transpose(0, 2, 1, 3)
    k_nope, v = kv[..., :NOPE], kv[..., NOPE:]
    k_rope = k_rope.reshape(B, 1, S, ROPE)
    c, si = f64(cos)[:, None], f64(sin)[:, None]
    k_rope = k_rope * c + rotate_half(k_rope) * si
    k_rope = np.broadcast_to(k_rope, (B, NH, S, ROPE))
    kk = np.concatenate([k_nope, k_rope], axis=-1)
    return kk, np.ascontiguousarray(v)


def e4m3fn_bytes(y):
    return np.clip(np.asarray(y, np.float64), -448.0, 448.0).astype(np.float32).astype(ml_dtypes.float8_e4m3fn).view(np.uint8)


def e4m3fn_values(b):
    return np.asarray(b, np.uint8).view(ml_dtypes.float8_e4m3fn).astype(np.float64)


def setup_inputs():
    d = draw0()
    x0 = np.asarray(d['hidden_states']).astype(np.float64)
    s = (np.max(np.abs(x0), axis=(0, 1), keepdims=True) / 448.0).astype(np.float32)
    out = {}
    for k, v in d.items():
        if k == 'hidden_states':
            out['hidden_states_bytes'] = e4m3fn_bytes(x0 / s.astype(np.float64))
            out['hidden_states_scale'] = s
        else:
            out[k] = v
    return out


def reference(hidden_states_bytes, hidden_states_scale, cos, sin, Wkva_words, Wkva_scales, bkva, Wkvb_words, Wkvb_scales):
    return core(e4m3fn_values(hidden_states_bytes) * hidden_states_scale.astype(np.float64), cos, sin, Wkva_words, Wkva_scales, bkva, Wkvb_words, Wkvb_scales)

from contextlib import ExitStack

import concourse.mybir as mybir
from concourse.masks import make_identity

S = 8192
K = 512
KV = 512
ROPE = 128
NOPE = 64
VD = 128
HEADS = 2
P = 128
J = 4
GROUP = P * J
GROUPS = S // GROUP

FLOPS = 2 * S * K * (KV + ROPE) + 2 * S * KV * HEADS * (NOPE + VD)

F32 = mybir.dt.float32
BF16 = mybir.dt.bfloat16
U32 = mybir.dt.uint32
I32 = mybir.dt.int32
U8 = mybir.dt.uint8
FP8 = mybir.dt.float8_e4m3fn
FP8X4 = mybir.dt.float8_e4m3fn_x4
FP4X4 = mybir.dt.float4_e2m1fn_x4
MULT = mybir.AluOpType.mult
ADD = mybir.AluOpType.add
SUB = mybir.AluOpType.subtract
IDENTITY = mybir.ActivationFunctionType.Identity


def tile_gptossmlaattention_pa_t_w4_kernel(
    tc, x_bytes, x_scale, cos, sin, wa_words, wa_scales, bkva, wb_words, wb_scales, out_k, out_v
):
    nc = tc.nc

    x_view = x_bytes[0].rearrange("(g p j) k -> g p (j k)", p=P, j=J)
    cos_view = cos[0].rearrange("(g p j) d -> g p (j d)", p=P, j=J)
    sin_view = sin[0].rearrange("(g p j) d -> g p (j d)", p=P, j=J)
    k_view = out_k[0].rearrange("h (g p j) d -> h g p j d", p=P, j=J)
    v_view = out_v[0].rearrange("h (g p j) d -> g p h (j d)", p=P, j=J)

    with ExitStack() as ctx:
        const = ctx.enter_context(tc.tile_pool(name="const", bufs=1))
        loads = ctx.enter_context(tc.tile_pool(name="loads", bufs=4))
        tables = ctx.enter_context(tc.tile_pool(name="tables", bufs=6))
        work = ctx.enter_context(tc.tile_pool(name="work", bufs=2))
        outs = ctx.enter_context(tc.tile_pool(name="outs", bufs=3))
        psum_x = ctx.enter_context(tc.psum_pool(name="psum_x", bufs=2))
        psum_k = ctx.enter_context(tc.psum_pool(name="psum_k", bufs=1))
        psum_a = ctx.enter_context(tc.psum_pool(name="psum_a", bufs=3))
        psum_b = ctx.enter_context(tc.psum_pool(name="psum_b", bufs=2))

        ctx.enter_context(tc.manual_schedule())

        x_raw = {}
        cos_t = {}
        sin_t = {}

        def load_x(g):
            xr = loads.tile([P, J * K], U8, align_bytes=64)
            half = J * K // 2
            if g == 0:
                nc.sync.dma_start(out=xr[:, :half], in_=x_view[g][:, :half])
                nc.sync.dma_start(out=xr[:, half:], in_=x_view[g][:, half:])
            else:
                nc.sync.dma_start(out=xr[:], in_=x_view[g])
            x_raw[g] = xr

        def load_tables(g):
            ct = tables.tile([P, J * ROPE], BF16, align_bytes=64)
            st = tables.tile([P, J * ROPE], BF16, align_bytes=64)
            nc.sync.dma_start(out=ct[:], in_=cos_view[g])
            nc.sync.dma_start(out=st[:], in_=sin_view[g])
            cos_t[g] = ct
            sin_t[g] = st

        scale = const.tile([P, 2 * K], F32, align_bytes=64)
        nc.scalar.dma_start(out=scale[:, :K], in_=x_scale.rearrange("b o k -> (b o k)").partition_broadcast(P))
        load_x(0)

        sa_raw = const.tile([P, KV + ROPE], U8, align_bytes=64)
        sb_raw = const.tile([P, HEADS * (NOPE + VD)], U8, align_bytes=64)
        nc.gpsimd.memset(sa_raw[:].bitcast(I32), 0)
        nc.gpsimd.memset(sb_raw[:].bitcast(I32), 0)
        ident = const.tile([P, P], F32, align_bytes=64)
        make_identity(nc, ident[:])

        wa_raw = const.tile([P, 2 * (KV + ROPE)], U8, align_bytes=64)
        nc.sync.dma_start(out=wa_raw[:], in_=wa_words[0])
        load_x(1)
        for r in range(4):
            nc.sync.dma_start(
                out=sa_raw[:].bitcast(I32)[r:P:32, :],
                in_=wa_scales[0].bitcast(I32).rearrange("(q r) n -> r q n", r=4)[r],
            )
        bias_bf = const.tile([P, 8], BF16, align_bytes=64)
        nc.sync.dma_start(out=bias_bf[:, 0:4], in_=bkva[0:KV].rearrange("(p t) -> p t", t=4))
        bias_rope_bf = const.tile([P, 8], BF16, align_bytes=64)
        nc.sync.dma_start(out=bias_rope_bf[:, 0:1], in_=bkva[KV : KV + ROPE].rearrange("(p t) -> p t", t=1))
        for r in range(4):
            nc.sync.dma_start(
                out=sb_raw[:].bitcast(I32)[r:P:32, :],
                in_=wb_scales[0].bitcast(I32).rearrange("(q r) n -> r q n", r=4)[r],
            )
        wv = const.tile([P, HEADS, 2 * VD], U8, align_bytes=64)
        wn = const.tile([P, HEADS, 2 * NOPE], U8, align_bytes=64)
        wb_view = wb_words[0].rearrange("p (h n) -> p h n", h=HEADS)
        nc.sync.dma_start(out=wn[:], in_=wb_view[:, :, 0 : 2 * NOPE])
        nc.sync.dma_start(out=wv[:], in_=wb_view[:, :, 2 * NOPE :])
        load_tables(0)
        load_x(2)
        load_tables(1)
        load_x(3)
        load_tables(2)
        load_tables(3)

        nc.scalar.copy(out=scale[:, K:], in_=scale[:, :K])

        bias = const.tile([P, 8], F32, align_bytes=64)
        nc.gpsimd.tensor_copy(out=bias[:, 0:4], in_=bias_bf[:, 0:4])
        bias_rope = const.tile([P, 8], F32, align_bytes=64)
        nc.gpsimd.tensor_copy(out=bias_rope[:, 0:1], in_=bias_rope_bf[:, 0:1])
        sa = const.tile([P, KV], U8, align_bytes=64)
        nc.gpsimd.tensor_copy(
            out=sa[:].rearrange("p (t m) -> p t m", t=4), in_=sa_raw[:, :KV].rearrange("p (m t) -> p t m", t=4)
        )
        sv = const.tile([P, HEADS, VD], U8, align_bytes=64)
        sn = const.tile([P, HEADS, NOPE], U8, align_bytes=64)
        sb_view = sb_raw[:].rearrange("p (h n) -> p h n", h=HEADS)
        nc.gpsimd.tensor_copy(out=sn[:], in_=sb_view[:, :, :NOPE])
        nc.gpsimd.tensor_copy(out=sv[:], in_=sb_view[:, :, NOPE:])
        wa = const.tile([P, 2 * KV], U8, align_bytes=64)

        wv_flat = wv[:].rearrange("p h n -> p (h n)")
        wn_flat = wn[:].rearrange("p h n -> p (h n)")
        sv_flat = sv[:].rearrange("p h n -> p (h n)")
        sn_flat = sn[:].rearrange("p h n -> p (h n)")

        x_wide = {}
        x_psum = {}
        x_words = {}
        x_codes = {}
        planes = {}
        rope_t = {}
        rope_psum = {}
        kv_codes = {}
        k_out = {}
        n_out = {}
        v_out = {}
        prods = {}
        v_psum = {}

        def widen(g, h):
            if h == 0:
                xw = work.tile([P, J * K], BF16, align_bytes=64)
                x_wide[g] = xw
            xw = x_wide[g]
            half = J * K // 2
            cols = slice(h * half, (h + 1) * half)
            nc.vector.tensor_tensor(
                out=xw[:, cols], in0=x_raw[g][:, cols].bitcast(FP8), in1=scale[:], op=MULT
            )

        def transpose_x(g):
            words = x_wide[g][:].bitcast(F32)
            x_psum[g] = []
            for h in range(2):
                xt = psum_x.tile([P, 2, 2, P], F32)
                for jj in range(2):
                    w0 = (2 * h + jj) * (K // 2)
                    for u in range(2):
                        nc.tensor.transpose(xt[:, jj, u, :], words[:, w0 + u : w0 + K // 2 : 2], ident[:])
                x_psum[g].append(xt)

        def unload_x(g):
            xg = work.tile([P, GROUP, 4], BF16, align_bytes=64)
            x_words[g] = xg
            xg_words = xg[:].rearrange("p n t -> p (n t)").bitcast(F32)
            for h in range(2):
                nc.scalar.copy(
                    out=xg_words[:, h * GROUP : (h + 1) * GROUP].rearrange("p (j n u) -> p j n u", j=2, u=2),
                    in_=x_psum[g][h][:].rearrange("p j u n -> p j n u"),
                )

        def quantize_x(g):
            xc = work.tile([P, GROUP], U32, align_bytes=64)
            xs = work.tile([P, GROUP], U8, align_bytes=64)
            nc.vector.quantize_mx(
                out=xc[:].bitcast(FP8X4), scales=xs[:], in_=x_words[g][:].rearrange("p n t -> p (n t)")
            )
            x_codes[g] = (xc, xs)

        def latent(g):
            xc, xs = x_codes[g]
            lp = work.tile([P, 4, GROUP], BF16, align_bytes=64)
            kt = work.tile([P, GROUP], F32, align_bytes=64)
            planes[g] = lp
            rope_t[g] = kt
            for t in (4, 0, 1, 2, 3):
                acc = psum_a.tile([P, GROUP], F32)
                if t == 4:
                    lhs = wa_raw[:, 2 * KV :]
                    lhs_scale = sa_raw[:, KV:]
                else:
                    lhs = wa[:, 256 * t : 256 * (t + 1)]
                    lhs_scale = sa[:, P * t : P * (t + 1)]
                nc.tensor.matmul_mx(
                    out=acc[:], lhsT=lhs.bitcast(FP4X4), lhsT_scale=lhs_scale,
                    rhs=xc[:].bitcast(FP8X4), rhs_scale=xs[:], start=True, stop=True,
                )
                if t == 4:
                    nc.scalar.activation(out=kt[:], in_=acc[:], func=IDENTITY, bias=bias_rope[:, 0:1])
                else:
                    nc.scalar.activation(out=lp[:, t, :], in_=acc[:], func=IDENTITY, bias=bias[:, t : t + 1])

        def transpose_rope(g):
            kp = psum_k.tile([P, J, ROPE], F32)
            for j in range(J):
                nc.tensor.transpose(kp[:, j, :], rope_t[g][:, j * P : (j + 1) * P], ident[:])
            rope_psum[g] = kp

        lat_wide = {}

        def interleave(g):
            lg = work.tile([P, GROUP, 4], BF16, align_bytes=64)
            nc.vector.tensor_copy(
                out=lg[:].rearrange("p (c i) t -> p c t i", i=4),
                in_=planes[g][:].rearrange("p t (c i) -> p c t i", i=4),
            )
            lat_wide[g] = lg

        def quantize_latent(g):
            lc = work.tile([P, GROUP], U32, align_bytes=64)
            ls = work.tile([P, GROUP], U8, align_bytes=64)
            nc.vector.quantize_mx(
                out=lc[:].bitcast(FP8X4), scales=ls[:], in_=lat_wide[g][:].rearrange("p n t -> p (n t)")
            )
            kv_codes[g] = (lc, ls)

        def rotate_products(g):
            t1 = work.tile([P, J, ROPE], F32, align_bytes=64)
            t2 = work.tile([P, J, ROPE], F32, align_bytes=64)
            kp = rope_psum[g]
            ct = cos_t[g][:].rearrange("p (j d) -> p j d", j=J)
            st = sin_t[g][:].rearrange("p (j d) -> p j d", j=J)
            hd = ROPE // 2
            nc.vector.tensor_tensor(out=t2[:, :, :hd], in0=kp[:, :, hd:], in1=st[:, :, :hd], op=MULT)
            nc.vector.tensor_tensor(out=t2[:, :, hd:], in0=kp[:, :, :hd], in1=st[:, :, hd:], op=MULT)
            nc.vector.tensor_tensor(out=t1[:], in0=kp[:], in1=ct, op=MULT)
            prods[g] = (t1, t2)

        def rotate_sum(g):
            t1, t2 = prods[g]
            hd = ROPE // 2
            ko = outs.tile([P, J, NOPE + ROPE], F32, align_bytes=64)
            k_out[g] = ko
            nc.vector.tensor_tensor(out=ko[:, :, NOPE : NOPE + hd], in0=t1[:, :, :hd], in1=t2[:, :, :hd], op=SUB)
            nc.vector.tensor_tensor(out=ko[:, :, NOPE + hd :], in0=t1[:, :, hd:], in1=t2[:, :, hd:], op=ADD)
            nc.sync.dma_start(out=k_view[1][g][:, :, NOPE:], in_=ko[:, :, NOPE:])

        def keys_values(g):
            lc, ls = kv_codes[g]
            vo = outs.tile([P, HEADS, J, VD], F32, align_bytes=64)
            no = outs.tile([P, J, NOPE], F32, align_bytes=64)
            ko = k_out[g]
            for half in range(2):
                vp = psum_b.tile([P, 512], F32, name="kv_psum")
                for jj in range(2):
                    j = 2 * half + jj
                    nc.tensor.matmul_mx(
                        out=vp[:, 256 * jj : 256 * (jj + 1)],
                        lhsT=lc[:, P * j : P * (j + 1)].bitcast(FP8X4), lhsT_scale=ls[:, P * j : P * (j + 1)],
                        rhs=wv_flat.bitcast(FP4X4), rhs_scale=sv_flat, start=True, stop=True,
                    )
                nc.scalar.copy(
                    out=vo[:, :, 2 * half : 2 * half + 2, :],
                    in_=vp[:].rearrange("p (j h d) -> p h j d", j=2, h=HEADS),
                )
            nc.sync.dma_start(out=v_view[g], in_=vo[:].rearrange("p h j d -> p h (j d)"))
            np_ = psum_b.tile([P, 512], F32, name="kv_psum")
            for j in range(J):
                nc.tensor.matmul_mx(
                    out=np_[:, P * j : P * (j + 1)],
                    lhsT=lc[:, P * j : P * (j + 1)].bitcast(FP8X4), lhsT_scale=ls[:, P * j : P * (j + 1)],
                    rhs=wn_flat.bitcast(FP4X4), rhs_scale=sn_flat, start=True, stop=True,
                )
            np_view = np_[:].rearrange("p (j h d) -> p j h d", j=J, h=HEADS)
            nc.scalar.copy(out=ko[:, :, :NOPE], in_=np_view[:, :, 0, :])
            nc.scalar.copy(out=no[:], in_=np_view[:, :, 1, :])
            nc.sync.dma_start(out=k_view[0][g], in_=ko[:])
            nc.sync.dma_start(out=k_view[1][g][:, :, :NOPE], in_=no[:])

        def ok(g):
            return 0 <= g < GROUPS

        for i in range(-2, GROUPS + 1):
            if ok(i + 1):
                unload_x(i + 1)
            if ok(i + 2):
                widen(i + 2, 0)
            if ok(i + 1):
                quantize_x(i + 1)
            if ok(i + 2):
                widen(i + 2, 1)
            if i == -2:
                nc.vector.tensor_copy(
                    out=wa[:].rearrange("p (t m c) -> p t m c", t=4, c=2),
                    in_=wa_raw[:, : 2 * KV].rearrange("p (m t c) -> p t m c", t=4, c=2),
                )
            if ok(i - 1):
                keys_values(i - 1)
            if ok(i + 1):
                latent(i + 1)
            if ok(i):
                interleave(i)
                if i < GROUPS - 1:
                    rotate_products(i)
                    quantize_latent(i)
                else:
                    quantize_latent(i)
                    rotate_products(i)
                rotate_sum(i)
            if ok(i + 4) and i + 4 > 3:
                load_x(i + 4)
                load_tables(i + 4)
            if ok(i + 2):
                transpose_x(i + 2)
            if ok(i + 1):
                transpose_rope(i + 1)
